import numpy as np
import ml_dtypes

BF16 = ml_dtypes.bfloat16


def bf(x):
    return np.asarray(x, np.float32).astype(BF16)


def f32(x):
    return np.asarray(x, np.float32)


def f64(x):
    return np.asarray(x).astype(np.float64)


def striped(idx):
    return np.tile(idx.reshape(-1, 16).T, (8, 1))


E, S, N, H, M = 1024, 256, 512, 512, 128


def setup_inputs():
    return {"emb": f32(np.random.standard_normal((E, S))), "pos": f32(np.random.standard_normal((E, 1))), "wh1": bf(np.random.standard_normal((E, H)) / np.sqrt(E)), "bh1": f32(0.1 * np.random.standard_normal((H, 1))), "wh2": bf(np.random.standard_normal((H, M)) / np.sqrt(H)), "bh2": f32(0.1 * np.random.standard_normal((M, 1))), "offs": striped(np.random.permutation(np.tile(np.arange(S), 2))[:N])}


def reference(emb, pos, wh1, bh1, wh2, bh2, offs):
    idx = offs[:16].T.reshape(-1)
    t = f64(emb)[:, idx] + f64(pos)
    y = np.maximum(f64(wh1).T @ t + f64(bh1), 0.0)
    return f64(wh2).T @ y + f64(bh2)

@@ -1,0 +1,80 @@
+import concourse.mybir as mybir
+
+F32, BF16, U16 = mybir.dt.float32, mybir.dt.bfloat16, mybir.dt.uint16
+ADD, MAX = mybir.AluOpType.add, mybir.AluOpType.max
+RELU = mybir.ActivationFunctionType.Relu
+IDENTITY = mybir.ActivationFunctionType.Identity
+
+P = 128
+E, S, N, H, M = 1024, 256, 512, 512, 128
+EB = E // P
+HB = H // P
+PIECE = S
+PIECES = N // PIECE
+
+FLOPS = 2 * N * (E * H + H * M)
+
+
+def tile_performerbaseline_kernel(tc, emb, pos, wh1, bh1, wh2, bh2, offs, out):
+    nc = tc.nc
+    with (
+        tc.tile_pool(name="held", bufs=1) as held,
+        tc.tile_pool(name="work", bufs=4) as work,
+        tc.psum_pool(name="psum", bufs=1) as psum,
+    ):
+        emb_blocks = emb.rearrange("(p b) s -> p b s", b=EB)
+        wh1_blocks = wh1.rearrange("(p b) h -> p b h", b=EB)
+
+        offsets = held.tile([P, N // 16], U16, name="offsets")
+        nc.sync.dma_start(offsets[:], offs)
+        pos_sb = held.tile([P, EB], F32, name="pos_sb")
+        nc.sync.dma_start(pos_sb[:], pos.rearrange("(p b) o -> p (b o)", b=EB))
+
+        windows = [held.tile([P, S], F32, name=f"window{b}") for b in range(EB)]
+        wh1_sb = [held.tile([P, H], BF16, name=f"wh1_sb{b}") for b in range(EB)]
+        for b in range(EB):
+            nc.scalar.dma_start(windows[b][:], emb_blocks[:, b, :])
+            nc.sync.dma_start(wh1_sb[b][:], wh1_blocks[:, b, :])
+
+        wh2_sb = held.tile([P, HB, M], BF16, name="wh2_sb")
+        nc.sync.dma_start(wh2_sb[:], wh2.rearrange("(p c) m -> p c m", c=HB))
+        bh1_sb = held.tile([P, HB], F32, name="bh1_sb")
+        nc.sync.dma_start(bh1_sb[:], bh1.rearrange("(p c) o -> p (c o)", c=HB))
+        bh2_sb = held.tile([P, 1], F32, name="bh2_sb")
+        nc.sync.dma_start(bh2_sb[:], bh2)
+
+        pos_rows = [held.tile([P, PIECE], F32, name=f"pos_rows{b}") for b in range(EB)]
+        for b in range(EB):
+            nc.gpsimd.tensor_copy(pos_rows[b][:], pos_sb[:, b : b + 1].to_broadcast([P, PIECE]))
+
+        y_ps = [psum.tile([P, N], F32, name=f"y_ps{c}") for c in range(HB)]
+        for b in range(EB):
+            t_bf = work.tile([P, N], BF16, name="t_bf")
+            for i in range(PIECES):
+                cols = slice(i * PIECE, (i + 1) * PIECE)
+                t32 = work.tile([P, PIECE], F32, name="t32")
+                nc.vector.tensor_tensor(
+                    t32[:],
+                    windows[b][:].indirect(offsets[:, i * (PIECE // 16) : (i + 1) * (PIECE // 16)]),
+                    pos_rows[b][:],
+                    ADD,
+                )
+                nc.scalar.copy(t_bf[:, cols], t32[:])
+            wh1_by_block = wh1_sb[b][:].rearrange("p (m c) -> p c m", c=HB)
+            for c in range(HB):
+                nc.tensor.matmul(
+                    y_ps[c][:], wh1_by_block[:, c, :], t_bf[:], start=(b == 0), stop=(b == EB - 1)
+                )
+
+        o_ps = psum.tile([P, N], F32, name="o_ps")
+        for c in range(HB):
+            y_bf = work.tile([P, N], BF16, name="y_bf")
+            if c % 2 == 0:
+                nc.scalar.activation(y_bf[:], y_ps[c][:], RELU, bias=bh1_sb[:, c : c + 1])
+            else:
+                nc.vector.tensor_scalar(y_bf[:], y_ps[c][:], bh1_sb[:, c : c + 1], 0.0, ADD, MAX)
+            nc.tensor.matmul(o_ps[:], wh2_sb[:, c, :], y_bf[:], start=(c == 0), stop=(c == HB - 1))
+
+        out_sb = held.tile([P, N], F32, name="out_sb")
+        nc.scalar.activation(out_sb[:], o_ps[:], IDENTITY, bias=bh2_sb[:])
+        nc.sync.dma_start(out, out_sb[:])

@@ -43,6 +43,10 @@ def tile_performerbaseline_kernel(tc, emb, pos, wh1, bh1, wh2, bh2, offs, out):
         bh2_sb = held.tile([P, 1], F32, name="bh2_sb")
         nc.sync.dma_start(bh2_sb[:], bh2)
 
+        table_warmer = held.tile([P, 1], F32, name="table_warmer")
+        nc.vector.memset(table_warmer[:], 0.0)
+        nc.scalar.copy(table_warmer[:], table_warmer[:])
+
         pos_rows = [held.tile([P, PIECE], F32, name=f"pos_rows{b}") for b in range(EB)]
         for b in range(EB):
             nc.gpsimd.tensor_copy(pos_rows[b][:], pos_sb[:, b : b + 1].to_broadcast([P, PIECE]))

@@ -31,10 +31,12 @@ def tile_performerbaseline_kernel(tc, emb, pos, wh1, bh1, wh2, bh2, offs, out):
         nc.sync.dma_start(pos_sb[:], pos.rearrange("(p b) o -> p (b o)", b=EB))
 
         windows = [held.tile([P, S], F32, name=f"window{b}") for b in range(EB)]
-        wh1_sb = [held.tile([P, H], BF16, name=f"wh1_sb{b}") for b in range(EB)]
+        wh1_sb = [held.tile([P, 2, H], BF16, name=f"wh1_sb{a}") for a in range(EB // 2)]
         for b in range(EB):
-            nc.scalar.dma_start(windows[b][:], emb_blocks[:, b, :])
-            nc.sync.dma_start(wh1_sb[b][:], wh1_blocks[:, b, :])
+            queue = nc.scalar if b == 0 else nc.sync
+            queue.dma_start(windows[b][:], emb_blocks[:, b, :])
+            if b % 2 == 0:
+                queue.dma_start(wh1_sb[b // 2][:], wh1_blocks[:, b : b + 2, :])
 
         wh2_sb = held.tile([P, HB, M], BF16, name="wh2_sb")
         nc.sync.dma_start(wh2_sb[:], wh2.rearrange("(p c) m -> p c m", c=HB))
@@ -64,7 +66,7 @@ def tile_performerbaseline_kernel(tc, emb, pos, wh1, bh1, wh2, bh2, offs, out):
                     ADD,
                 )
                 nc.scalar.copy(t_bf[:, cols], t32[:])
-            wh1_by_block = wh1_sb[b][:].rearrange("p (m c) -> p c m", c=HB)
+            wh1_by_block = wh1_sb[b // 2][:, b % 2, :].rearrange("p (m c) -> p c m", c=HB)
             for c in range(HB):
                 nc.tensor.matmul(
                     y_ps[c][:], wh1_by_block[:, c, :], t_bf[:], start=(b == 0), stop=(b == EB - 1)

@@ -11,6 +11,7 @@ EB = E // P
 HB = H // P
 PIECE = S
 PIECES = N // PIECE
+WARM_MATMULS = 10
 
 FLOPS = 2 * N * (E * H + H * M)
 
@@ -25,10 +26,10 @@ def tile_performerbaseline_kernel(tc, emb, pos, wh1, bh1, wh2, bh2, offs, out):
         emb_blocks = emb.rearrange("(p b) s -> p b s", b=EB)
         wh1_blocks = wh1.rearrange("(p b) h -> p b h", b=EB)
 
-        offsets = held.tile([P, N // 16], U16, name="offsets")
-        nc.sync.dma_start(offsets[:], offs)
         pos_sb = held.tile([P, EB], F32, name="pos_sb")
         nc.sync.dma_start(pos_sb[:], pos.rearrange("(p b) o -> p (b o)", b=EB))
+        offsets = held.tile([P, N // 16], U16, name="offsets")
+        nc.sync.dma_start(offsets[:], offs)
 
         windows = [held.tile([P, S], F32, name=f"window{b}") for b in range(EB)]
         wh1_sb = [held.tile([P, 2, H], BF16, name=f"wh1_sb{a}") for a in range(EB // 2)]
@@ -48,6 +49,12 @@ def tile_performerbaseline_kernel(tc, emb, pos, wh1, bh1, wh2, bh2, offs, out):
         table_warmer = held.tile([P, 1], F32, name="table_warmer")
         nc.vector.memset(table_warmer[:], 0.0)
         nc.scalar.copy(table_warmer[:], table_warmer[:])
+
+        zeros = held.tile([P, N], BF16, name="zeros")
+        nc.vector.memset(zeros[:], 0.0)
+        warm_ps = psum.tile([P, N], F32, name="warm_ps")
+        for _ in range(WARM_MATMULS):
+            nc.tensor.matmul(warm_ps[:], zeros[:, 0:P], zeros[:], start=True, stop=True)
 
         pos_rows = [held.tile([P, PIECE], F32, name=f"pos_rows{b}") for b in range(EB)]
         for b in range(EB):

@@ -57,11 +57,12 @@ def tile_performerbaseline_kernel(tc, emb, pos, wh1, bh1, wh2, bh2, offs, out):
             nc.tensor.matmul(warm_ps[:], zeros[:, 0:P], zeros[:], start=True, stop=True)
 
         pos_rows = [held.tile([P, PIECE], F32, name=f"pos_rows{b}") for b in range(EB)]
-        for b in range(EB):
-            nc.gpsimd.tensor_copy(pos_rows[b][:], pos_sb[:, b : b + 1].to_broadcast([P, PIECE]))
+        nc.scalar.copy(pos_rows[0][:], pos_sb[:, 0:1].to_broadcast([P, PIECE]))
 
         y_ps = [psum.tile([P, N], F32, name=f"y_ps{c}") for c in range(HB)]
         for b in range(EB):
+            if b + 1 < EB:
+                nc.scalar.copy(pos_rows[b + 1][:], pos_sb[:, b + 1 : b + 2].to_broadcast([P, PIECE]))
             t_bf = work.tile([P, N], BF16, name="t_bf")
             for i in range(PIECES):
                 cols = slice(i * PIECE, (i + 1) * PIECE)

@@ -40,9 +40,10 @@ def tile_performerbaseline_kernel(tc, emb, pos, wh1, bh1, wh2, bh2, offs, out):
                 queue.dma_start(wh1_sb[b // 2][:], wh1_blocks[:, b : b + 2, :])
 
         wh2_sb = held.tile([P, HB, M], BF16, name="wh2_sb")
-        nc.sync.dma_start(wh2_sb[:], wh2.rearrange("(p c) m -> p c m", c=HB))
+        nc.sync.dma_start(wh2_sb[:], wh2.rearrange("(c p) m -> p c m", p=P))
         bh1_sb = held.tile([P, HB], F32, name="bh1_sb")
-        nc.sync.dma_start(bh1_sb[:], bh1.rearrange("(p c) o -> p (c o)", c=HB))
+        with nc.allow_non_contiguous_dma(reason="512 biases, one to a partition and block"):
+            nc.sync.dma_start(bh1_sb[:], bh1.rearrange("(c p) o -> p (c o)", p=P))
         bh2_sb = held.tile([P, 1], F32, name="bh2_sb")
         nc.sync.dma_start(bh2_sb[:], bh2)
 
@@ -74,21 +75,33 @@ def tile_performerbaseline_kernel(tc, emb, pos, wh1, bh1, wh2, bh2, offs, out):
                     ADD,
                 )
                 nc.scalar.copy(t_bf[:, cols], t32[:])
-            wh1_by_block = wh1_sb[b // 2][:, b % 2, :].rearrange("p (m c) -> p c m", c=HB)
+            wh1_by_block = wh1_sb[b // 2][:, b % 2, :].rearrange("p (c m) -> p c m", c=HB)
             for c in range(HB):
                 nc.tensor.matmul(
                     y_ps[c][:], wh1_by_block[:, c, :], t_bf[:], start=(b == 0), stop=(b == EB - 1)
                 )
 
-        o_ps = psum.tile([P, N], F32, name="o_ps")
+        o_ps = [psum.tile([P, PIECE], F32, name=f"o_ps{i}") for i in range(PIECES)]
         for c in range(HB):
             y_bf = work.tile([P, N], BF16, name="y_bf")
             if c % 2 == 0:
                 nc.scalar.activation(y_bf[:], y_ps[c][:], RELU, bias=bh1_sb[:, c : c + 1])
             else:
                 nc.vector.tensor_scalar(y_bf[:], y_ps[c][:], bh1_sb[:, c : c + 1], 0.0, ADD, MAX)
-            nc.tensor.matmul(o_ps[:], wh2_sb[:, c, :], y_bf[:], start=(c == 0), stop=(c == HB - 1))
+            for i in range(PIECES):
+                nc.tensor.matmul(
+                    o_ps[i][:],
+                    wh2_sb[:, c, :],
+                    y_bf[:, i * PIECE : (i + 1) * PIECE],
+                    start=(c == 0),
+                    stop=(c == HB - 1),
+                )
 
-        out_sb = held.tile([P, N], F32, name="out_sb")
-        nc.scalar.activation(out_sb[:], o_ps[:], IDENTITY, bias=bh2_sb[:])
-        nc.sync.dma_start(out, out_sb[:])
+        for i in range(PIECES):
+            out_sb = held.tile([P, PIECE], F32, name=f"out_sb{i}")
+            if i % 2 == 0:
+                nc.scalar.activation(out_sb[:], o_ps[i][:], IDENTITY, bias=bh2_sb[:])
+                nc.scalar.dma_start(out[:, i * PIECE : (i + 1) * PIECE], out_sb[:])
+            else:
+                nc.vector.tensor_scalar(out_sb[:], o_ps[i][:], bh2_sb[:], None, ADD)
+                nc.sync.dma_start(out[:, i * PIECE : (i + 1) * PIECE], out_sb[:])

@@ -40,10 +40,9 @@ def tile_performerbaseline_kernel(tc, emb, pos, wh1, bh1, wh2, bh2, offs, out):
                 queue.dma_start(wh1_sb[b // 2][:], wh1_blocks[:, b : b + 2, :])
 
         wh2_sb = held.tile([P, HB, M], BF16, name="wh2_sb")
-        nc.sync.dma_start(wh2_sb[:], wh2.rearrange("(c p) m -> p c m", p=P))
+        nc.sync.dma_start(wh2_sb[:], wh2.rearrange("(p c) m -> p c m", c=HB))
         bh1_sb = held.tile([P, HB], F32, name="bh1_sb")
-        with nc.allow_non_contiguous_dma(reason="512 biases, one to a partition and block"):
-            nc.sync.dma_start(bh1_sb[:], bh1.rearrange("(c p) o -> p (c o)", p=P))
+        nc.sync.dma_start(bh1_sb[:], bh1.rearrange("(p c) o -> p (c o)", c=HB))
         bh2_sb = held.tile([P, 1], F32, name="bh2_sb")
         nc.sync.dma_start(bh2_sb[:], bh2)
 
@@ -75,7 +74,7 @@ def tile_performerbaseline_kernel(tc, emb, pos, wh1, bh1, wh2, bh2, offs, out):
                     ADD,
                 )
                 nc.scalar.copy(t_bf[:, cols], t32[:])
-            wh1_by_block = wh1_sb[b // 2][:, b % 2, :].rearrange("p (c m) -> p c m", c=HB)
+            wh1_by_block = wh1_sb[b // 2][:, b % 2, :].rearrange("p (m c) -> p c m", c=HB)
             for c in range(HB):
                 nc.tensor.matmul(
                     y_ps[c][:], wh1_by_block[:, c, :], t_bf[:], start=(b == 0), stop=(b == EB - 1)

@@ -3,7 +3,6 @@ import concourse.mybir as mybir
 F32, BF16, U16 = mybir.dt.float32, mybir.dt.bfloat16, mybir.dt.uint16
 ADD, MAX = mybir.AluOpType.add, mybir.AluOpType.max
 RELU = mybir.ActivationFunctionType.Relu
-IDENTITY = mybir.ActivationFunctionType.Identity
 
 P = 128
 E, S, N, H, M = 1024, 256, 512, 512, 128
@@ -11,7 +10,7 @@ EB = E // P
 HB = H // P
 PIECE = S
 PIECES = N // PIECE
-WARM_MATMULS = 10
+WARM_MATMULS = 8
 
 FLOPS = 2 * N * (E * H + H * M)
 
@@ -80,27 +79,15 @@ def tile_performerbaseline_kernel(tc, emb, pos, wh1, bh1, wh2, bh2, offs, out):
                     y_ps[c][:], wh1_by_block[:, c, :], t_bf[:], start=(b == 0), stop=(b == EB - 1)
                 )
 
-        o_ps = [psum.tile([P, PIECE], F32, name=f"o_ps{i}") for i in range(PIECES)]
+        o_ps = psum.tile([P, N], F32, name="o_ps")
         for c in range(HB):
             y_bf = work.tile([P, N], BF16, name="y_bf")
             if c % 2 == 0:
                 nc.scalar.activation(y_bf[:], y_ps[c][:], RELU, bias=bh1_sb[:, c : c + 1])
             else:
                 nc.vector.tensor_scalar(y_bf[:], y_ps[c][:], bh1_sb[:, c : c + 1], 0.0, ADD, MAX)
-            for i in range(PIECES):
-                nc.tensor.matmul(
-                    o_ps[i][:],
-                    wh2_sb[:, c, :],
-                    y_bf[:, i * PIECE : (i + 1) * PIECE],
-                    start=(c == 0),
-                    stop=(c == HB - 1),
-                )
+            nc.tensor.matmul(o_ps[:], wh2_sb[:, c, :], y_bf[:], start=(c == 0), stop=(c == HB - 1))
 
-        for i in range(PIECES):
-            out_sb = held.tile([P, PIECE], F32, name=f"out_sb{i}")
-            if i % 2 == 0:
-                nc.scalar.activation(out_sb[:], o_ps[i][:], IDENTITY, bias=bh2_sb[:])
-                nc.scalar.dma_start(out[:, i * PIECE : (i + 1) * PIECE], out_sb[:])
-            else:
-                nc.vector.tensor_scalar(out_sb[:], o_ps[i][:], bh2_sb[:], None, ADD)
-                nc.sync.dma_start(out[:, i * PIECE : (i + 1) * PIECE], out_sb[:])
+        out_sb = held.tile([P, N], F32, name="out_sb")
+        nc.vector.tensor_scalar(out_sb[:], o_ps[:], bh2_sb[:], None, ADD)
+        nc.sync.dma_start(out, out_sb[:])

@@ -3,14 +3,16 @@ import concourse.mybir as mybir
 F32, BF16, U16 = mybir.dt.float32, mybir.dt.bfloat16, mybir.dt.uint16
 ADD, MAX = mybir.AluOpType.add, mybir.AluOpType.max
 RELU = mybir.ActivationFunctionType.Relu
+IDENTITY = mybir.ActivationFunctionType.Identity
 
 P = 128
 E, S, N, H, M = 1024, 256, 512, 512, 128
 EB = E // P
 HB = H // P
-PIECE = S
-PIECES = N // PIECE
+HALF = S
+HALVES = N // HALF
 WARM_MATMULS = 8
+PSUM_BANKS = 8
 
 FLOPS = 2 * N * (E * H + H * M)
 
@@ -20,7 +22,7 @@ def tile_performerbaseline_kernel(tc, emb, pos, wh1, bh1, wh2, bh2, offs, out):
     with (
         tc.tile_pool(name="held", bufs=1) as held,
         tc.tile_pool(name="work", bufs=4) as work,
-        tc.psum_pool(name="psum", bufs=1) as psum,
+        tc.psum_pool(name="psum", bufs=PSUM_BANKS) as psum,
     ):
         emb_blocks = emb.rearrange("(p b) s -> p b s", b=EB)
         wh1_blocks = wh1.rearrange("(p b) h -> p b h", b=EB)
@@ -49,45 +51,84 @@ def tile_performerbaseline_kernel(tc, emb, pos, wh1, bh1, wh2, bh2, offs, out):
         nc.vector.memset(table_warmer[:], 0.0)
         nc.scalar.copy(table_warmer[:], table_warmer[:])
 
+        def psum_bank(columns, name):
+            return psum.tile([P, columns], F32, name=name, tag="bank")
+
         zeros = held.tile([P, N], BF16, name="zeros")
         nc.vector.memset(zeros[:], 0.0)
-        warm_ps = psum.tile([P, N], F32, name="warm_ps")
+        warm_ps = psum_bank(N, "warm_ps")
         for _ in range(WARM_MATMULS):
             nc.tensor.matmul(warm_ps[:], zeros[:, 0:P], zeros[:], start=True, stop=True)
 
-        pos_rows = [held.tile([P, PIECE], F32, name=f"pos_rows{b}") for b in range(EB)]
-        nc.scalar.copy(pos_rows[0][:], pos_sb[:, 0:1].to_broadcast([P, PIECE]))
+        pos_rows = [held.tile([P, HALF], F32, name=f"pos_rows{b}") for b in range(EB)]
 
-        y_ps = [psum.tile([P, N], F32, name=f"y_ps{c}") for c in range(HB)]
-        for b in range(EB):
-            if b + 1 < EB:
-                nc.scalar.copy(pos_rows[b + 1][:], pos_sb[:, b + 1 : b + 2].to_broadcast([P, PIECE]))
-            t_bf = work.tile([P, N], BF16, name="t_bf")
-            for i in range(PIECES):
-                cols = slice(i * PIECE, (i + 1) * PIECE)
-                t32 = work.tile([P, PIECE], F32, name="t32")
-                nc.vector.tensor_tensor(
-                    t32[:],
-                    windows[b][:].indirect(offsets[:, i * (PIECE // 16) : (i + 1) * (PIECE // 16)]),
-                    pos_rows[b][:],
-                    ADD,
-                )
-                nc.scalar.copy(t_bf[:, cols], t32[:])
+        def repeat_pos(b):
+            nc.scalar.copy(pos_rows[b][:], pos_sb[:, b : b + 1].to_broadcast([P, HALF]))
+
+        y_ps = {}
+        y_bf = {}
+        o_ps = {}
+
+        def layer1(i, b):
+            t32 = work.tile([P, HALF], F32, name="t32")
+            nc.vector.tensor_tensor(
+                t32[:],
+                windows[b][:].indirect(offsets[:, i * (HALF // 16) : (i + 1) * (HALF // 16)]),
+                pos_rows[b][:],
+                ADD,
+            )
+            t_bf = work.tile([P, HALF], BF16, name="t_bf")
+            nc.scalar.copy(t_bf[:], t32[:])
             wh1_by_block = wh1_sb[b // 2][:, b % 2, :].rearrange("p (m c) -> p c m", c=HB)
             for c in range(HB):
                 nc.tensor.matmul(
-                    y_ps[c][:], wh1_by_block[:, c, :], t_bf[:], start=(b == 0), stop=(b == EB - 1)
+                    y_ps[i, c][:], wh1_by_block[:, c, :], t_bf[:], start=(b == 0), stop=(b == EB - 1)
                 )
 
-        o_ps = psum.tile([P, N], F32, name="o_ps")
-        for c in range(HB):
-            y_bf = work.tile([P, N], BF16, name="y_bf")
-            if c % 2 == 0:
-                nc.scalar.activation(y_bf[:], y_ps[c][:], RELU, bias=bh1_sb[:, c : c + 1])
+        def relu(i, c, on_scalar):
+            y_bf[i, c] = held.tile([P, HALF], BF16, name=f"y_bf{i}_{c}")
+            if on_scalar:
+                nc.scalar.activation(y_bf[i, c][:], y_ps[i, c][:], RELU, bias=bh1_sb[:, c : c + 1])
             else:
-                nc.vector.tensor_scalar(y_bf[:], y_ps[c][:], bh1_sb[:, c : c + 1], 0.0, ADD, MAX)
-            nc.tensor.matmul(o_ps[:], wh2_sb[:, c, :], y_bf[:], start=(c == 0), stop=(c == HB - 1))
+                nc.vector.tensor_scalar(
+                    y_bf[i, c][:], y_ps[i, c][:], bh1_sb[:, c : c + 1], 0.0, ADD, MAX
+                )
 
-        out_sb = held.tile([P, N], F32, name="out_sb")
-        nc.vector.tensor_scalar(out_sb[:], o_ps[:], bh2_sb[:], None, ADD)
-        nc.sync.dma_start(out, out_sb[:])
+        def layer2(i, c):
+            if c == 0:
+                o_ps[i] = psum_bank(HALF, f"o_ps{i}")
+            nc.tensor.matmul(
+                o_ps[i][:], wh2_sb[:, c, :], y_bf[i, c][:], start=(c == 0), stop=(c == HB - 1)
+            )
+
+        def finish(i, on_scalar):
+            out_sb = held.tile([P, HALF], F32, name=f"out_sb{i}")
+            if on_scalar:
+                nc.scalar.activation(out_sb[:], o_ps[i][:], IDENTITY, bias=bh2_sb[:])
+            else:
+                nc.vector.tensor_scalar(out_sb[:], o_ps[i][:], bh2_sb[:], None, ADD)
+            nc.sync.dma_start(out[:, i * HALF : (i + 1) * HALF], out_sb[:])
+
+        repeat_pos(0)
+        for c in range(HB):
+            y_ps[0, c] = psum_bank(HALF, f"y_ps0_{c}")
+        for b in range(EB):
+            if b + 1 < EB:
+                repeat_pos(b + 1)
+            layer1(0, b)
+
+        for c in range(HB):
+            y_ps[1, c] = psum_bank(HALF, f"y_ps1_{c}")
+        for b in range(EB):
+            layer1(1, b)
+            if b < HB:
+                relu(0, b, on_scalar=True)
+            if 1 <= b <= HB:
+                layer2(0, b - 1)
+            if b == HB + 1:
+                finish(0, on_scalar=True)
+
+        for c in range(HB):
+            relu(1, c, on_scalar=(c % 2 == 0))
+            layer2(1, c)
+        finish(1, on_scalar=False)

@@ -13,6 +13,8 @@ HALF = S
 HALVES = N // HALF
 WARM_MATMULS = 8
 PSUM_BANKS = 8
+EARLY_BLOCKS = 2
+LAG = 1
 
 FLOPS = 2 * N * (E * H + H * M)
 
@@ -110,22 +112,28 @@ def tile_performerbaseline_kernel(tc, emb, pos, wh1, bh1, wh2, bh2, offs, out):
             nc.sync.dma_start(out[:, i * HALF : (i + 1) * HALF], out_sb[:])
 
         repeat_pos(0)
-        for c in range(HB):
-            y_ps[0, c] = psum_bank(HALF, f"y_ps0_{c}")
-        for b in range(EB):
+        for i in range(HALVES):
+            for c in range(HB):
+                y_ps[i, c] = psum_bank(HALF, f"y_ps{i}_{c}")
+
+        for b in range(EARLY_BLOCKS):
+            repeat_pos(b + 1)
+            for i in range(HALVES):
+                layer1(i, b)
+
+        for b in range(EARLY_BLOCKS, EB):
             if b + 1 < EB:
                 repeat_pos(b + 1)
             layer1(0, b)
 
-        for c in range(HB):
-            y_ps[1, c] = psum_bank(HALF, f"y_ps1_{c}")
-        for b in range(EB):
-            layer1(1, b)
-            if b < HB:
-                relu(0, b, on_scalar=True)
-            if 1 <= b <= HB:
-                layer2(0, b - 1)
-            if b == HB + 1:
+        for step in range(LAG + HB + 2):
+            if EARLY_BLOCKS + step < EB:
+                layer1(1, EARLY_BLOCKS + step)
+            if LAG <= step < LAG + HB:
+                relu(0, step - LAG, on_scalar=True)
+            if LAG + 1 <= step < LAG + 1 + HB:
+                layer2(0, step - LAG - 1)
+            if step == LAG + 1 + HB:
                 finish(0, on_scalar=True)
 
         for c in range(HB):

@@ -36,11 +36,10 @@ def tile_performerbaseline_kernel(tc, emb, pos, wh1, bh1, wh2, bh2, offs, out):
 
         windows = [held.tile([P, S], F32, name=f"window{b}") for b in range(EB)]
         wh1_sb = [held.tile([P, 2, H], BF16, name=f"wh1_sb{a}") for a in range(EB // 2)]
-        for b in range(EB):
-            queue = nc.scalar if b == 0 else nc.sync
-            queue.dma_start(windows[b][:], emb_blocks[:, b, :])
-            if b % 2 == 0:
-                queue.dma_start(wh1_sb[b // 2][:], wh1_blocks[:, b : b + 2, :])
+        for a in range(EB // 2):
+            for b in (2 * a, 2 * a + 1):
+                nc.sync.dma_start(windows[b][:], emb_blocks[:, b, :])
+            nc.sync.dma_start(wh1_sb[a][:], wh1_blocks[:, 2 * a : 2 * a + 2, :])
 
         wh2_sb = held.tile([P, HB, M], BF16, name="wh2_sb")
         nc.sync.dma_start(wh2_sb[:], wh2.rearrange("(p c) m -> p c m", c=HB))

@@ -13,7 +13,7 @@ HALF = S
 HALVES = N // HALF
 WARM_MATMULS = 8
 PSUM_BANKS = 8
-EARLY_BLOCKS = 2
+EARLY_BLOCKS = 3
 LAG = 1
 
 FLOPS = 2 * N * (E * H + H * M)

@@ -13,7 +13,7 @@ HALF = S
 HALVES = N // HALF
 WARM_MATMULS = 8
 PSUM_BANKS = 8
-EARLY_BLOCKS = 3
+EARLY_BLOCKS = 4
 LAG = 1
 
 FLOPS = 2 * N * (E * H + H * M)
@@ -47,10 +47,6 @@ def tile_performerbaseline_kernel(tc, emb, pos, wh1, bh1, wh2, bh2, offs, out):
         nc.sync.dma_start(bh1_sb[:], bh1.rearrange("(p c) o -> p (c o)", c=HB))
         bh2_sb = held.tile([P, 1], F32, name="bh2_sb")
         nc.sync.dma_start(bh2_sb[:], bh2)
-
-        table_warmer = held.tile([P, 1], F32, name="table_warmer")
-        nc.vector.memset(table_warmer[:], 0.0)
-        nc.scalar.copy(table_warmer[:], table_warmer[:])
 
         def psum_bank(columns, name):
             return psum.tile([P, columns], F32, name=name, tag="bank")

@@ -11,7 +11,6 @@ EB = E // P
 HB = H // P
 HALF = S
 HALVES = N // HALF
-WARM_MATMULS = 8
 PSUM_BANKS = 8
 EARLY_BLOCKS = 4
 LAG = 1
@@ -50,12 +49,6 @@ def tile_performerbaseline_kernel(tc, emb, pos, wh1, bh1, wh2, bh2, offs, out):
 
         def psum_bank(columns, name):
             return psum.tile([P, columns], F32, name=name, tag="bank")
-
-        zeros = held.tile([P, N], BF16, name="zeros")
-        nc.vector.memset(zeros[:], 0.0)
-        warm_ps = psum_bank(N, "warm_ps")
-        for _ in range(WARM_MATMULS):
-            nc.tensor.matmul(warm_ps[:], zeros[:, 0:P], zeros[:], start=True, stop=True)
 
         pos_rows = [held.tile([P, HALF], F32, name=f"pos_rows{b}") for b in range(EB)]
 

@@ -115,14 +115,15 @@ def tile_performerbaseline_kernel(tc, emb, pos, wh1, bh1, wh2, bh2, offs, out):
             layer1(0, b)
 
         for step in range(LAG + HB + 2):
-            if EARLY_BLOCKS + step < EB:
+            gathering = EARLY_BLOCKS + step < EB
+            if gathering:
                 layer1(1, EARLY_BLOCKS + step)
             if LAG <= step < LAG + HB:
-                relu(0, step - LAG, on_scalar=True)
+                relu(0, step - LAG, on_scalar=gathering)
             if LAG + 1 <= step < LAG + 1 + HB:
                 layer2(0, step - LAG - 1)
             if step == LAG + 1 + HB:
-                finish(0, on_scalar=True)
+                finish(0, on_scalar=gathering)
 
         for c in range(HB):
             relu(1, c, on_scalar=(c % 2 == 0))

@@ -31,14 +31,15 @@ def tile_performerbaseline_kernel(tc, emb, pos, wh1, bh1, wh2, bh2, offs, out):
         pos_sb = held.tile([P, EB], F32, name="pos_sb")
         nc.sync.dma_start(pos_sb[:], pos.rearrange("(p b) o -> p (b o)", b=EB))
         offsets = held.tile([P, N // 16], U16, name="offsets")
-        nc.sync.dma_start(offsets[:], offs)
 
         windows = [held.tile([P, S], F32, name=f"window{b}") for b in range(EB)]
         wh1_sb = [held.tile([P, 2, H], BF16, name=f"wh1_sb{a}") for a in range(EB // 2)]
         for a in range(EB // 2):
-            for b in (2 * a, 2 * a + 1):
-                nc.sync.dma_start(windows[b][:], emb_blocks[:, b, :])
+            nc.sync.dma_start(windows[2 * a][:], emb_blocks[:, 2 * a, :])
+            if a == 0:
+                nc.sync.dma_start(offsets[:], offs)
             nc.sync.dma_start(wh1_sb[a][:], wh1_blocks[:, 2 * a : 2 * a + 2, :])
+            nc.sync.dma_start(windows[2 * a + 1][:], emb_blocks[:, 2 * a + 1, :])
 
         wh2_sb = held.tile([P, HB, M], BF16, name="wh2_sb")
         nc.sync.dma_start(wh2_sb[:], wh2.rearrange("(p c) m -> p c m", c=HB))
@@ -53,7 +54,11 @@ def tile_performerbaseline_kernel(tc, emb, pos, wh1, bh1, wh2, bh2, offs, out):
         pos_rows = [held.tile([P, HALF], F32, name=f"pos_rows{b}") for b in range(EB)]
 
         def repeat_pos(b):
-            nc.scalar.copy(pos_rows[b][:], pos_sb[:, b : b + 1].to_broadcast([P, HALF]))
+            row = pos_sb[:, b : b + 1].to_broadcast([P, HALF])
+            if b == 0:
+                nc.vector.tensor_copy(pos_rows[b][:], row)
+            else:
+                nc.scalar.copy(pos_rows[b][:], row)
 
         y_ps = {}
         y_bf = {}

@@ -3,7 +3,6 @@ import concourse.mybir as mybir
 F32, BF16, U16 = mybir.dt.float32, mybir.dt.bfloat16, mybir.dt.uint16
 ADD, MAX = mybir.AluOpType.add, mybir.AluOpType.max
 RELU = mybir.ActivationFunctionType.Relu
-IDENTITY = mybir.ActivationFunctionType.Identity
 
 P = 128
 E, S, N, H, M = 1024, 256, 512, 512, 128
@@ -13,6 +12,7 @@ HALF = S
 HALVES = N // HALF
 PSUM_BANKS = 8
 EARLY_BLOCKS = 4
+WARM_UPS = 4
 LAG = 1
 
 FLOPS = 2 * N * (E * H + H * M)
@@ -50,6 +50,12 @@ def tile_performerbaseline_kernel(tc, emb, pos, wh1, bh1, wh2, bh2, offs, out):
 
         def psum_bank(columns, name):
             return psum.tile([P, columns], F32, name=name, tag="bank")
+
+        zeros = held.tile([P, 512], BF16, name="zeros")
+        nc.vector.memset(zeros[:], 0.0)
+        warm_ps = psum_bank(512, "warm_ps")
+        for w in range(WARM_UPS):
+            nc.tensor.matmul(warm_ps[:], zeros[:, :P], zeros[:], start=True, stop=True)
 
         pos_rows = [held.tile([P, HALF], F32, name=f"pos_rows{b}") for b in range(EB)]
 
@@ -96,41 +102,36 @@ def tile_performerbaseline_kernel(tc, emb, pos, wh1, bh1, wh2, bh2, offs, out):
                 o_ps[i][:], wh2_sb[:, c, :], y_bf[i, c][:], start=(c == 0), stop=(c == HB - 1)
             )
 
-        def finish(i, on_scalar):
+        def finish(i):
             out_sb = held.tile([P, HALF], F32, name=f"out_sb{i}")
-            if on_scalar:
-                nc.scalar.activation(out_sb[:], o_ps[i][:], IDENTITY, bias=bh2_sb[:])
-            else:
-                nc.vector.tensor_scalar(out_sb[:], o_ps[i][:], bh2_sb[:], None, ADD)
+            nc.vector.tensor_scalar(out_sb[:], o_ps[i][:], bh2_sb[:], None, ADD)
             nc.sync.dma_start(out[:, i * HALF : (i + 1) * HALF], out_sb[:])
 
-        repeat_pos(0)
+        for b in range(EARLY_BLOCKS):
+            repeat_pos(b)
         for i in range(HALVES):
             for c in range(HB):
                 y_ps[i, c] = psum_bank(HALF, f"y_ps{i}_{c}")
 
         for b in range(EARLY_BLOCKS):
-            repeat_pos(b + 1)
             for i in range(HALVES):
                 layer1(i, b)
+            repeat_pos(EARLY_BLOCKS + b)
 
         for b in range(EARLY_BLOCKS, EB):
-            if b + 1 < EB:
-                repeat_pos(b + 1)
             layer1(0, b)
 
         for step in range(LAG + HB + 2):
-            gathering = EARLY_BLOCKS + step < EB
-            if gathering:
+            if EARLY_BLOCKS + step < EB:
                 layer1(1, EARLY_BLOCKS + step)
             if LAG <= step < LAG + HB:
-                relu(0, step - LAG, on_scalar=gathering)
+                relu(0, step - LAG, on_scalar=(step - LAG < HB // 2))
             if LAG + 1 <= step < LAG + 1 + HB:
                 layer2(0, step - LAG - 1)
             if step == LAG + 1 + HB:
-                finish(0, on_scalar=gathering)
+                finish(0)
 
         for c in range(HB):
             relu(1, c, on_scalar=(c % 2 == 0))
             layer2(1, c)
-        finish(1, on_scalar=False)
+        finish(1)

@@ -22,6 +22,7 @@ def tile_performerbaseline_kernel(tc, emb, pos, wh1, bh1, wh2, bh2, offs, out):
     nc = tc.nc
     with (
         tc.tile_pool(name="held", bufs=1) as held,
+        tc.tile_pool(name="sums", bufs=HALVES * EB) as sums,
         tc.tile_pool(name="work", bufs=4) as work,
         tc.psum_pool(name="psum", bufs=PSUM_BANKS) as psum,
     ):
@@ -71,7 +72,7 @@ def tile_performerbaseline_kernel(tc, emb, pos, wh1, bh1, wh2, bh2, offs, out):
         o_ps = {}
 
         def layer1(i, b):
-            t32 = work.tile([P, HALF], F32, name="t32")
+            t32 = sums.tile([P, HALF], F32, name="t32")
             nc.vector.tensor_tensor(
                 t32[:],
                 windows[b][:].indirect(offsets[:, i * (HALF // 16) : (i + 1) * (HALF // 16)]),

@@ -13,7 +13,6 @@ HALVES = N // HALF
 PSUM_BANKS = 8
 EARLY_BLOCKS = 4
 WARM_UPS = 4
-LAG = 1
 
 FLOPS = 2 * N * (E * H + H * M)
 
@@ -122,17 +121,15 @@ def tile_performerbaseline_kernel(tc, emb, pos, wh1, bh1, wh2, bh2, offs, out):
         for b in range(EARLY_BLOCKS, EB):
             layer1(0, b)
 
-        for step in range(LAG + HB + 2):
-            if EARLY_BLOCKS + step < EB:
-                layer1(1, EARLY_BLOCKS + step)
-            if LAG <= step < LAG + HB:
-                relu(0, step - LAG, on_scalar=(step - LAG < HB // 2))
-            if LAG + 1 <= step < LAG + 1 + HB:
-                layer2(0, step - LAG - 1)
-            if step == LAG + 1 + HB:
-                finish(0)
+        for b in range(EARLY_BLOCKS, EB):
+            layer1(1, b)
+        for c in range(HB):
+            relu(0, c, on_scalar=False)
+            layer2(0, c)
 
         for c in range(HB):
             relu(1, c, on_scalar=(c % 2 == 0))
+        finish(0)
+        for c in range(HB):
             layer2(1, c)
         finish(1)

@@ -33,13 +33,12 @@ def tile_performerbaseline_kernel(tc, emb, pos, wh1, bh1, wh2, bh2, offs, out):
         offsets = held.tile([P, N // 16], U16, name="offsets")
 
         windows = [held.tile([P, S], F32, name=f"window{b}") for b in range(EB)]
-        wh1_sb = [held.tile([P, 2, H], BF16, name=f"wh1_sb{a}") for a in range(EB // 2)]
-        for a in range(EB // 2):
-            nc.sync.dma_start(windows[2 * a][:], emb_blocks[:, 2 * a, :])
-            if a == 0:
+        wh1_sb = [held.tile([P, H], BF16, name=f"wh1_sb{b}") for b in range(EB)]
+        for b in range(EB):
+            nc.sync.dma_start(windows[b][:], emb_blocks[:, b, :])
+            if b == 0:
                 nc.sync.dma_start(offsets[:], offs)
-            nc.sync.dma_start(wh1_sb[a][:], wh1_blocks[:, 2 * a : 2 * a + 2, :])
-            nc.sync.dma_start(windows[2 * a + 1][:], emb_blocks[:, 2 * a + 1, :])
+            nc.sync.dma_start(wh1_sb[b][:], wh1_blocks[:, b, :])
 
         wh2_sb = held.tile([P, HB, M], BF16, name="wh2_sb")
         nc.sync.dma_start(wh2_sb[:], wh2.rearrange("(p c) m -> p c m", c=HB))
@@ -80,7 +79,7 @@ def tile_performerbaseline_kernel(tc, emb, pos, wh1, bh1, wh2, bh2, offs, out):
             )
             t_bf = work.tile([P, HALF], BF16, name="t_bf")
             nc.scalar.copy(t_bf[:], t32[:])
-            wh1_by_block = wh1_sb[b // 2][:, b % 2, :].rearrange("p (m c) -> p c m", c=HB)
+            wh1_by_block = wh1_sb[b][:].rearrange("p (m c) -> p c m", c=HB)
             for c in range(HB):
                 nc.tensor.matmul(
                     y_ps[i, c][:], wh1_by_block[:, c, :], t_bf[:], start=(b == 0), stop=(b == EB - 1)

@@ -3,6 +3,7 @@ import concourse.mybir as mybir
 F32, BF16, U16 = mybir.dt.float32, mybir.dt.bfloat16, mybir.dt.uint16
 ADD, MAX = mybir.AluOpType.add, mybir.AluOpType.max
 RELU = mybir.ActivationFunctionType.Relu
+IDENTITY = mybir.ActivationFunctionType.Identity
 
 P = 128
 E, S, N, H, M = 1024, 256, 512, 512, 128
@@ -12,7 +13,6 @@ HALF = S
 HALVES = N // HALF
 PSUM_BANKS = 8
 EARLY_BLOCKS = 4
-WARM_UPS = 4
 
 FLOPS = 2 * N * (E * H + H * M)
 
@@ -49,12 +49,6 @@ def tile_performerbaseline_kernel(tc, emb, pos, wh1, bh1, wh2, bh2, offs, out):
 
         def psum_bank(columns, name):
             return psum.tile([P, columns], F32, name=name, tag="bank")
-
-        zeros = held.tile([P, 512], BF16, name="zeros")
-        nc.vector.memset(zeros[:], 0.0)
-        warm_ps = psum_bank(512, "warm_ps")
-        for w in range(WARM_UPS):
-            nc.tensor.matmul(warm_ps[:], zeros[:, :P], zeros[:], start=True, stop=True)
 
         pos_rows = [held.tile([P, HALF], F32, name=f"pos_rows{b}") for b in range(EB)]
 
@@ -94,16 +88,28 @@ def tile_performerbaseline_kernel(tc, emb, pos, wh1, bh1, wh2, bh2, offs, out):
                     y_bf[i, c][:], y_ps[i, c][:], bh1_sb[:, c : c + 1], 0.0, ADD, MAX
                 )
 
-        def layer2(i, c):
-            if c == 0:
-                o_ps[i] = psum_bank(HALF, f"o_ps{i}")
-            nc.tensor.matmul(
-                o_ps[i][:], wh2_sb[:, c, :], y_bf[i, c][:], start=(c == 0), stop=(c == HB - 1)
-            )
+        def layer2(i, c, parts):
+            columns = HALF // parts
+            for q in range(parts):
+                if c == 0:
+                    o_ps[i, q] = psum_bank(columns, f"o_ps{i}_{q}")
+                nc.tensor.matmul(
+                    o_ps[i, q][:],
+                    wh2_sb[:, c, :],
+                    y_bf[i, c][:, q * columns : (q + 1) * columns],
+                    start=(c == 0),
+                    stop=(c == HB - 1),
+                )
 
-        def finish(i):
+        def finish(i, parts):
             out_sb = held.tile([P, HALF], F32, name=f"out_sb{i}")
-            nc.vector.tensor_scalar(out_sb[:], o_ps[i][:], bh2_sb[:], None, ADD)
+            columns = HALF // parts
+            for q in range(parts):
+                part = out_sb[:, q * columns : (q + 1) * columns]
+                if q < parts - 1:
+                    nc.scalar.activation(part, o_ps[i, q][:], IDENTITY, bias=bh2_sb[:])
+                else:
+                    nc.vector.tensor_scalar(part, o_ps[i, q][:], bh2_sb[:], None, ADD)
             nc.sync.dma_start(out[:, i * HALF : (i + 1) * HALF], out_sb[:])
 
         for b in range(EARLY_BLOCKS):
@@ -124,11 +130,11 @@ def tile_performerbaseline_kernel(tc, emb, pos, wh1, bh1, wh2, bh2, offs, out):
             layer1(1, b)
         for c in range(HB):
             relu(0, c, on_scalar=False)
-            layer2(0, c)
+            layer2(0, c, parts=1)
 
         for c in range(HB):
             relu(1, c, on_scalar=(c % 2 == 0))
-        finish(0)
+        finish(0, parts=1)
         for c in range(HB):
-            layer2(1, c)
-        finish(1)
+            layer2(1, c, parts=2)
+        finish(1, parts=2)

@@ -3,7 +3,6 @@ import concourse.mybir as mybir
 F32, BF16, U16 = mybir.dt.float32, mybir.dt.bfloat16, mybir.dt.uint16
 ADD, MAX = mybir.AluOpType.add, mybir.AluOpType.max
 RELU = mybir.ActivationFunctionType.Relu
-IDENTITY = mybir.ActivationFunctionType.Identity
 
 P = 128
 E, S, N, H, M = 1024, 256, 512, 512, 128
@@ -41,9 +40,9 @@ def tile_performerbaseline_kernel(tc, emb, pos, wh1, bh1, wh2, bh2, offs, out):
             nc.sync.dma_start(wh1_sb[b][:], wh1_blocks[:, b, :])
 
         wh2_sb = held.tile([P, HB, M], BF16, name="wh2_sb")
-        nc.sync.dma_start(wh2_sb[:], wh2.rearrange("(p c) m -> p c m", c=HB))
+        nc.sync.dma_start(wh2_sb[:], wh2.rearrange("(c p) m -> p c m", c=HB))
         bh1_sb = held.tile([P, HB], F32, name="bh1_sb")
-        nc.sync.dma_start(bh1_sb[:], bh1.rearrange("(p c) o -> p (c o)", c=HB))
+        nc.sync.dma_start(bh1_sb[:], bh1.rearrange("(c p) o -> p (c o)", c=HB))
         bh2_sb = held.tile([P, 1], F32, name="bh2_sb")
         nc.sync.dma_start(bh2_sb[:], bh2)
 
@@ -73,10 +72,13 @@ def tile_performerbaseline_kernel(tc, emb, pos, wh1, bh1, wh2, bh2, offs, out):
             )
             t_bf = work.tile([P, HALF], BF16, name="t_bf")
             nc.scalar.copy(t_bf[:], t32[:])
-            wh1_by_block = wh1_sb[b][:].rearrange("p (m c) -> p c m", c=HB)
             for c in range(HB):
                 nc.tensor.matmul(
-                    y_ps[i, c][:], wh1_by_block[:, c, :], t_bf[:], start=(b == 0), stop=(b == EB - 1)
+                    y_ps[i, c][:],
+                    wh1_sb[b][:, c * P : (c + 1) * P],
+                    t_bf[:],
+                    start=(b == 0),
+                    stop=(b == EB - 1),
                 )
 
         def relu(i, c, on_scalar):
@@ -88,28 +90,16 @@ def tile_performerbaseline_kernel(tc, emb, pos, wh1, bh1, wh2, bh2, offs, out):
                     y_bf[i, c][:], y_ps[i, c][:], bh1_sb[:, c : c + 1], 0.0, ADD, MAX
                 )
 
-        def layer2(i, c, parts):
-            columns = HALF // parts
-            for q in range(parts):
-                if c == 0:
-                    o_ps[i, q] = psum_bank(columns, f"o_ps{i}_{q}")
-                nc.tensor.matmul(
-                    o_ps[i, q][:],
-                    wh2_sb[:, c, :],
-                    y_bf[i, c][:, q * columns : (q + 1) * columns],
-                    start=(c == 0),
-                    stop=(c == HB - 1),
-                )
+        def layer2(i, c):
+            if c == 0:
+                o_ps[i] = psum_bank(HALF, f"o_ps{i}")
+            nc.tensor.matmul(
+                o_ps[i][:], wh2_sb[:, c, :], y_bf[i, c][:], start=(c == 0), stop=(c == HB - 1)
+            )
 
-        def finish(i, parts):
+        def finish(i):
             out_sb = held.tile([P, HALF], F32, name=f"out_sb{i}")
-            columns = HALF // parts
-            for q in range(parts):
-                part = out_sb[:, q * columns : (q + 1) * columns]
-                if q < parts - 1:
-                    nc.scalar.activation(part, o_ps[i, q][:], IDENTITY, bias=bh2_sb[:])
-                else:
-                    nc.vector.tensor_scalar(part, o_ps[i, q][:], bh2_sb[:], None, ADD)
+            nc.vector.tensor_scalar(out_sb[:], o_ps[i][:], bh2_sb[:], None, ADD)
             nc.sync.dma_start(out[:, i * HALF : (i + 1) * HALF], out_sb[:])
 
         for b in range(EARLY_BLOCKS):
@@ -130,11 +120,11 @@ def tile_performerbaseline_kernel(tc, emb, pos, wh1, bh1, wh2, bh2, offs, out):
             layer1(1, b)
         for c in range(HB):
             relu(0, c, on_scalar=False)
-            layer2(0, c, parts=1)
+            layer2(0, c)
 
         for c in range(HB):
             relu(1, c, on_scalar=(c % 2 == 0))
-        finish(0, parts=1)
+        finish(0)
         for c in range(HB):
-            layer2(1, c, parts=2)
-        finish(1, parts=2)
+            layer2(1, c)
+        finish(1)

import concourse.mybir as mybir

F32, BF16, U16 = mybir.dt.float32, mybir.dt.bfloat16, mybir.dt.uint16
ADD, MAX = mybir.AluOpType.add, mybir.AluOpType.max
RELU = mybir.ActivationFunctionType.Relu

P = 128
E, S, N, H, M = 1024, 256, 512, 512, 128
EB = E // P
HB = H // P
HALF = S
HALVES = N // HALF
PSUM_BANKS = 8
EARLY_BLOCKS = 4

FLOPS = 2 * N * (E * H + H * M)


def tile_performerbaseline_kernel(tc, emb, pos, wh1, bh1, wh2, bh2, offs, out):
    nc = tc.nc
    with (
        tc.tile_pool(name="held", bufs=1) as held,
        tc.tile_pool(name="sums", bufs=HALVES * EB) as sums,
        tc.tile_pool(name="work", bufs=4) as work,
        tc.psum_pool(name="psum", bufs=PSUM_BANKS) as psum,
    ):
        emb_blocks = emb.rearrange("(p b) s -> p b s", b=EB)
        wh1_blocks = wh1.rearrange("(p b) h -> p b h", b=EB)

        pos_sb = held.tile([P, EB], F32, name="pos_sb")
        nc.sync.dma_start(pos_sb[:], pos.rearrange("(p b) o -> p (b o)", b=EB))
        offsets = held.tile([P, N // 16], U16, name="offsets")

        windows = [held.tile([P, S], F32, name=f"window{b}") for b in range(EB)]
        wh1_sb = [held.tile([P, H], BF16, name=f"wh1_sb{b}") for b in range(EB)]
        for b in range(EB):
            nc.sync.dma_start(windows[b][:], emb_blocks[:, b, :])
            if b == 0:
                nc.sync.dma_start(offsets[:], offs)
            nc.sync.dma_start(wh1_sb[b][:], wh1_blocks[:, b, :])

        wh2_sb = held.tile([P, HB, M], BF16, name="wh2_sb")
        nc.sync.dma_start(wh2_sb[:], wh2.rearrange("(c p) m -> p c m", c=HB))
        bh1_sb = held.tile([P, HB], F32, name="bh1_sb")
        nc.sync.dma_start(bh1_sb[:], bh1.rearrange("(c p) o -> p (c o)", c=HB))
        bh2_sb = held.tile([P, 1], F32, name="bh2_sb")
        nc.sync.dma_start(bh2_sb[:], bh2)

        def psum_bank(columns, name):
            return psum.tile([P, columns], F32, name=name, tag="bank")

        pos_rows = [held.tile([P, HALF], F32, name=f"pos_rows{b}") for b in range(EB)]

        def repeat_pos(b):
            row = pos_sb[:, b : b + 1].to_broadcast([P, HALF])
            if b == 0:
                nc.vector.tensor_copy(pos_rows[b][:], row)
            else:
                nc.scalar.copy(pos_rows[b][:], row)

        y_ps = {}
        y_bf = {}
        o_ps = {}

        def layer1(i, b):
            t32 = sums.tile([P, HALF], F32, name="t32")
            nc.vector.tensor_tensor(
                t32[:],
                windows[b][:].indirect(offsets[:, i * (HALF // 16) : (i + 1) * (HALF // 16)]),
                pos_rows[b][:],
                ADD,
            )
            t_bf = work.tile([P, HALF], BF16, name="t_bf")
            nc.scalar.copy(t_bf[:], t32[:])
            for c in range(HB):
                nc.tensor.matmul(
                    y_ps[i, c][:],
                    wh1_sb[b][:, c * P : (c + 1) * P],
                    t_bf[:],
                    start=(b == 0),
                    stop=(b == EB - 1),
                )

        def relu(i, c, on_scalar):
            y_bf[i, c] = held.tile([P, HALF], BF16, name=f"y_bf{i}_{c}")
            if on_scalar:
                nc.scalar.activation(y_bf[i, c][:], y_ps[i, c][:], RELU, bias=bh1_sb[:, c : c + 1])
            else:
                nc.vector.tensor_scalar(
                    y_bf[i, c][:], y_ps[i, c][:], bh1_sb[:, c : c + 1], 0.0, ADD, MAX
                )

        def layer2(i, c):
            if c == 0:
                o_ps[i] = psum_bank(HALF, f"o_ps{i}")
            nc.tensor.matmul(
                o_ps[i][:], wh2_sb[:, c, :], y_bf[i, c][:], start=(c == 0), stop=(c == HB - 1)
            )

        def finish(i):
            out_sb = held.tile([P, HALF], F32, name=f"out_sb{i}")
            nc.vector.tensor_scalar(out_sb[:], o_ps[i][:], bh2_sb[:], None, ADD)
            nc.sync.dma_start(out[:, i * HALF : (i + 1) * HALF], out_sb[:])

        for b in range(EARLY_BLOCKS):
            repeat_pos(b)
        for i in range(HALVES):
            for c in range(HB):
                y_ps[i, c] = psum_bank(HALF, f"y_ps{i}_{c}")

        for b in range(EARLY_BLOCKS):
            for i in range(HALVES):
                layer1(i, b)
            repeat_pos(EARLY_BLOCKS + b)

        for b in range(EARLY_BLOCKS, EB):
            layer1(0, b)

        for b in range(EARLY_BLOCKS, EB):
            layer1(1, b)
        for c in range(HB):
            relu(0, c, on_scalar=False)
            layer2(0, c)

        for c in range(HB):
            relu(1, c, on_scalar=(c % 2 == 0))
        finish(0)
        for c in range(HB):
            layer2(1, c)
        finish(1)
